import numpy as np
import ml_dtypes


def mxq(x, axis, fmt="e4m3"):
    dtype, down = {"e4m3": (ml_dtypes.float8_e4m3fn, 7), "e5m2": (ml_dtypes.float8_e5m2, 14)}[fmt]
    v = np.moveaxis(np.asarray(x, np.float32).astype(ml_dtypes.bfloat16).astype(np.float64), axis, -1)
    blocks = v.reshape(v.shape[:-1] + (-1, 32))
    amax = np.abs(blocks).max(-1, keepdims=True)
    byte = np.maximum(np.where(amax > 0, np.frexp(amax)[1] - 1 + 127, 0) - down, 1)
    scale = np.exp2(byte - 127.0)
    codes = (blocks / scale).astype(np.float32).astype(dtype).astype(np.float64)
    return np.moveaxis((codes * scale).reshape(v.shape), -1, axis)


WIDE = False


def mx_kscale(k):
    if not WIDE:
        return np.ones(k)
    levels = np.array([10, -10, 5, -5, 0])
    a = np.random.permutation(np.resize(levels, k // 512 * 4)).reshape(k // 512, 4)
    idx = np.arange(k)
    return np.exp2(a[idx // 512, idx % 128 // 32])


BF16 = ml_dtypes.bfloat16


def bf(x):
    return np.asarray(x, np.float32).astype(BF16)


def f64(x):
    return np.asarray(x).astype(np.float64)


B, N, D, F1, F2, F3, G1, G2 = 4, 32, 512, 512, 1024, 512, 512, 512
ALPHA = 0.2


def lrelu(v):
    return np.maximum(v, ALPHA * v)


def setup_inputs():
    s, t = mx_kscale(F2), mx_kscale(F3 + D)
    return {"e2": bf(lrelu(np.random.standard_normal((B, N, N, F2))) * s),
            "x": bf(np.random.standard_normal((B, N, D)) * t[F3:]),
            "fe_w2": bf(np.random.standard_normal((F2, F3)) * (12.0 / N) / np.sqrt(F2) / s[:, None] * t[:F3]),
            "fe_b2": bf(np.random.standard_normal(F3) * (3.0 / N) * t[:F3]),
            "fn_w0": bf(np.random.standard_normal((F3 + D, G1)) * 0.25 / np.sqrt(F3 + D) / t[:, None]),
            "fn_b0": bf(np.random.standard_normal(G1) * 0.3)}


def reference(e2, x, fe_w2, fe_b2, fn_w0, fn_b0):
    a3 = lrelu((mxq(f64(e2), 3, "e4m3") @ mxq(f64(fe_w2), 0, "e4m3")) + f64(fe_b2))
    agg = a3.sum(axis=2)
    h = np.concatenate([agg, f64(x)], axis=-1)
    return lrelu((mxq(h, 2, "e4m3") @ mxq(f64(fn_w0), 0, "e4m3")) + f64(fn_b0))

@@ -1,0 +1,242 @@
+from contextlib import ExitStack
+
+import concourse.mybir as mybir
+from concourse.masks import make_identity
+
+F32 = mybir.dt.float32
+BF16 = mybir.dt.bfloat16
+U32 = mybir.dt.uint32
+U8 = mybir.dt.uint8
+FP8X4 = mybir.dt.float8_e4m3fn_x4
+ALU = mybir.AluOpType
+ACT = mybir.ActivationFunctionType
+AXIS = mybir.AxisListType
+
+P = 128
+PACK = 4
+K_PASS = P * PACK
+NODES = 128
+NEIGHBOURS = 32
+K = 1024
+PASSES = K // K_PASS
+WIDTH = 512
+F_TILES = WIDTH // P
+J_CHUNK = 4
+CHUNKS = NEIGHBOURS // J_CHUNK
+COLS = J_CHUNK * NODES
+WORD_BLOCKS = K // 2 // P
+ALPHA = 0.2
+GPSIMD_TILES = 3
+
+FLOPS = 2 * NODES * NEIGHBOURS * K * WIDTH + 2 * NODES * K * WIDTH
+
+
+def quantise_weight(nc, pool, raw, codes, scales):
+    grouped = []
+    for g in range(PASSES):
+        tile_g = pool.tile([P, WIDTH * PACK], BF16, align_bytes=64, name="w_grouped_%d" % g)
+        nc.vector.tensor_copy(
+            out=tile_g[:].rearrange("p (c i t) -> p c t i", i=4, t=PACK),
+            in_=raw[:, g * PACK : (g + 1) * PACK, :].rearrange("p t (c i) -> p c t i", i=4),
+        )
+        grouped.append(tile_g)
+    for g in range(PASSES):
+        nc.vector.quantize_mx(
+            out=codes[:, g, :].bitcast(FP8X4), scales=scales[:, g, :], in_=grouped[g][:]
+        )
+
+
+def tile_graph_gan_pb_kernel(tc, e2, x, fe_w2, fe_b2, fn_w0, fn_b0, out):
+    nc = tc.nc
+    with ExitStack() as stack:
+        keep = stack.enter_context(tc.tile_pool(name="keep", bufs=1))
+        w_stage = stack.enter_context(tc.tile_pool(name="w_stage", bufs=2))
+        stage = stack.enter_context(tc.tile_pool(name="stage", bufs=3))
+        work = stack.enter_context(tc.tile_pool(name="work", bufs=4))
+        psum_t = stack.enter_context(tc.psum_pool(name="psum_t", bufs=4))
+        psum_acc = stack.enter_context(tc.psum_pool(name="psum_acc", bufs=4))
+
+        ident_f32 = keep.tile([P, P], F32)
+        make_identity(nc, ident_f32[:])
+        ident_bf16 = keep.tile([P, P], BF16)
+        make_identity(nc, ident_bf16[:])
+
+        b2_rows = keep.tile([P, P], BF16)
+        nc.vector.memset(b2_rows[:], 0.0)
+        nc.scalar.dma_start(out=b2_rows[0:F_TILES, :], in_=fe_b2.rearrange("(t p) -> t p", p=P))
+        x_sb = keep.tile([P, K_PASS], BF16)
+        nc.scalar.dma_start(out=x_sb[:], in_=x.rearrange("b i d -> (b i) d"))
+
+        w1_raw = keep.tile([P, PASSES * PACK, WIDTH], BF16)
+        nc.sync.dma_start(
+            out=w1_raw[:].rearrange("p (a e) c -> p a e c", e=2),
+            in_=fe_w2.rearrange("(a p e) c -> p a e c", p=P, e=2),
+        )
+        e2_rows = e2.rearrange("b i j k -> (b i) (j k)")
+        e2_sb = []
+        w0_raw = keep.tile([P, PASSES * PACK, WIDTH], BF16)
+        for c in range(CHUNKS):
+            e2_c = keep.tile([P, J_CHUNK * K], BF16, name="e2_%d" % c)
+            nc.sync.dma_start(out=e2_c[:], in_=e2_rows[:, c * J_CHUNK * K : (c + 1) * J_CHUNK * K])
+            e2_sb.append(e2_c)
+            if c == 0:
+                nc.sync.dma_start(out=w0_raw[:], in_=fn_w0.rearrange("(a p) c -> p a c", p=P))
+        b0_all = keep.tile([P, WIDTH], BF16)
+        nc.sync.dma_start(out=b0_all[:], in_=fn_b0.partition_broadcast(P))
+
+        w1_codes = keep.tile([P, PASSES, WIDTH], U32, align_bytes=64)
+        w1_scales = keep.tile([P, PASSES, WIDTH], U8, align_bytes=64)
+        quantise_weight(nc, w_stage, w1_raw, w1_codes, w1_scales)
+        w0_codes = keep.tile([P, PASSES, WIDTH], U32, align_bytes=64)
+        w0_scales = keep.tile([P, PASSES, WIDTH], U8, align_bytes=64)
+        quantise_weight(nc, w_stage, w0_raw, w0_codes, w0_scales)
+
+        b2_ps = psum_t.tile([P, P], BF16, tag="xt")
+        nc.tensor.transpose(b2_ps[:], b2_rows[:], ident_bf16[:])
+        b2 = keep.tile([P, F_TILES], F32)
+        nc.vector.tensor_copy(out=b2[:], in_=b2_ps[:, 0:F_TILES])
+        b2_alpha = keep.tile([P, F_TILES], F32)
+        nc.vector.tensor_scalar_mul(out=b2_alpha[:], in0=b2[:], scalar1=ALPHA)
+        b2_neg = keep.tile([P, F_TILES], F32)
+        nc.vector.tensor_scalar_mul(out=b2_neg[:], in0=b2[:], scalar1=-1.0)
+        b2_all_j = keep.tile([P, F_TILES], F32)
+        nc.vector.tensor_scalar_mul(out=b2_all_j[:], in0=b2[:], scalar1=float(NEIGHBOURS))
+
+        h_grouped = keep.tile([P, PASSES * NODES * PACK], BF16, align_bytes=64)
+        h_view = h_grouped[:].rearrange("p (g n t) -> p g n t", g=PASSES, t=PACK)
+        h_codes = keep.tile([P, PASSES, NODES], U32, align_bytes=64)
+        h_scales = keep.tile([P, PASSES, NODES], U8, align_bytes=64)
+
+        def quantise_h(g):
+            nc.vector.quantize_mx(
+                out=h_codes[:, g, :].bitcast(FP8X4),
+                scales=h_scales[:, g, :],
+                in_=h_grouped[:, g * NODES * PACK : (g + 1) * NODES * PACK],
+            )
+
+        x_ps = psum_t.tile([P, PACK, NODES], BF16, tag="xt")
+        for t in range(PACK):
+            nc.tensor.transpose(x_ps[:, t, :], x_sb[:, t * P : (t + 1) * P], ident_bf16[:])
+        nc.vector.tensor_copy(out=h_view[:, 1, :, :], in_=x_ps[:].rearrange("p t n -> p n t"))
+        quantise_h(1)
+
+        def quantise_chunk(c):
+            e2_words = e2_sb[c][:].bitcast(F32)
+            grouped = stage.tile([P, PASSES * COLS * PACK], BF16, align_bytes=64)
+            grouped_words = grouped[:].bitcast(F32).rearrange(
+                "p (g j n u) -> p g j n u", g=PASSES, j=J_CHUNK, u=2
+            )
+            for j in range(J_CHUNK):
+                xt = psum_t.tile([P, WORD_BLOCKS, NODES], F32)
+                for w in range(WORD_BLOCKS):
+                    first = (j * WORD_BLOCKS + w) * P
+                    nc.tensor.transpose(xt[:, w, :], e2_words[:, first : first + P], ident_f32[:])
+                nc.scalar.copy(
+                    out=grouped_words[:, :, j, :, :],
+                    in_=xt[:].rearrange("p (g u) n -> p g n u", u=2),
+                )
+            codes = stage.tile([P, PASSES, COLS], U32, align_bytes=64)
+            scales = stage.tile([P, PASSES, COLS], U8, align_bytes=64)
+            nc.vector.quantize_mx(
+                out=codes[:].rearrange("p g c -> p (g c)").bitcast(FP8X4),
+                scales=scales[:].rearrange("p g c -> p (g c)"),
+                in_=grouped[:],
+            )
+            return codes, scales
+
+        a3_sum = [keep.tile([P, COLS], F32, name="a3_sum_%d" % t) for t in range(GPSIMD_TILES)]
+        vector_tiles = range(GPSIMD_TILES, F_TILES)
+        v_sum = dict((t, keep.tile([P, COLS], F32, name="v_sum_%d" % t)) for t in vector_tiles)
+        clip_sum = dict((t, keep.tile([P, COLS], F32, name="clip_sum_%d" % t)) for t in vector_tiles)
+
+        def edge_layer(c, codes, scales):
+            for t in range(F_TILES):
+                f_cols = slice(t * P, (t + 1) * P)
+                acc = psum_acc.tile([P, COLS], F32)
+                for g in range(PASSES):
+                    nc.tensor.matmul_mx(
+                        out=acc[:],
+                        lhsT=w1_codes[:, g, f_cols].bitcast(FP8X4),
+                        lhsT_scale=w1_scales[:, g, f_cols],
+                        rhs=codes[:, g, :].bitcast(FP8X4),
+                        rhs_scale=scales[:, g, :],
+                        start=(g == 0),
+                        stop=(g == PASSES - 1),
+                    )
+                if t < GPSIMD_TILES:
+                    scaled = work.tile([P, COLS], F32)
+                    nc.scalar.activation(
+                        out=scaled[:], in_=acc[:], func=ACT.Identity,
+                        bias=b2_alpha[:, t : t + 1], scale=ALPHA,
+                    )
+                    a3 = a3_sum[t] if c == 0 else work.tile([P, COLS], F32, name="a3")
+                    nc.vector.scalar_tensor_tensor(
+                        out=a3[:], in0=acc[:], scalar=b2[:, t : t + 1], in1=scaled[:],
+                        op0=ALU.add, op1=ALU.max,
+                    )
+                    if c > 0:
+                        nc.gpsimd.tensor_tensor(
+                            out=a3_sum[t][:], in0=a3_sum[t][:], in1=a3[:], op=ALU.add
+                        )
+                elif c == 0:
+                    nc.vector.tensor_copy(out=v_sum[t][:], in_=acc[:])
+                    nc.vector.tensor_scalar_max(
+                        out=clip_sum[t][:], in0=acc[:], scalar1=b2_neg[:, t : t + 1]
+                    )
+                else:
+                    nc.vector.tensor_tensor(
+                        out=v_sum[t][:], in0=acc[:], in1=v_sum[t][:], op=ALU.add
+                    )
+                    nc.vector.scalar_tensor_tensor(
+                        out=clip_sum[t][:], in0=acc[:], scalar=b2_neg[:, t : t + 1],
+                        in1=clip_sum[t][:], op0=ALU.max, op1=ALU.add,
+                    )
+
+        ready = quantise_chunk(0)
+        for c in range(CHUNKS):
+            following = quantise_chunk(c + 1) if c + 1 < CHUNKS else None
+            edge_layer(c, ready[0], ready[1])
+            ready = following
+
+        for t in range(F_TILES):
+            agg = work.tile([P, NODES], F32)
+            if t < GPSIMD_TILES:
+                nc.vector.tensor_reduce(
+                    out=agg[:], in_=a3_sum[t][:].rearrange("p (j n) -> p n j", j=J_CHUNK),
+                    axis=AXIS.X, op=ALU.add,
+                )
+                nc.vector.tensor_copy(out=h_view[:, 0, :, t], in_=agg[:])
+            else:
+                both = work.tile([P, COLS], F32)
+                nc.vector.scalar_tensor_tensor(
+                    out=both[:], in0=clip_sum[t][:], scalar=(1.0 - ALPHA) / ALPHA,
+                    in1=v_sum[t][:], op0=ALU.mult, op1=ALU.add,
+                )
+                nc.vector.tensor_reduce(
+                    out=agg[:], in_=both[:].rearrange("p (j n) -> p n j", j=J_CHUNK),
+                    axis=AXIS.X, op=ALU.add,
+                )
+                nc.vector.tensor_scalar(
+                    out=h_view[:, 0, :, t], in0=agg[:], scalar1=ALPHA,
+                    scalar2=b2_all_j[:, t : t + 1], op0=ALU.mult, op1=ALU.add,
+                )
+        quantise_h(0)
+
+        out_ps = psum_acc.tile([P, WIDTH], F32, tag="acc")
+        for g in range(PASSES):
+            nc.tensor.matmul_mx(
+                out=out_ps[:],
+                lhsT=h_codes[:, g, :].bitcast(FP8X4),
+                lhsT_scale=h_scales[:, g, :],
+                rhs=w0_codes[:, g, :].bitcast(FP8X4),
+                rhs_scale=w0_scales[:, g, :],
+                start=(g == 0),
+                stop=(g == PASSES - 1),
+            )
+        biased = keep.tile([P, WIDTH], F32)
+        nc.vector.tensor_tensor(out=biased[:], in0=out_ps[:], in1=b0_all[:], op=ALU.add)
+        result = keep.tile([P, WIDTH], F32)
+        nc.vector.scalar_tensor_tensor(
+            out=result[:], in0=biased[:], scalar=ALPHA, in1=biased[:], op0=ALU.mult, op1=ALU.max
+        )
+        nc.sync.dma_start(out=out.rearrange("b i g -> (b i) g"), in_=result[:])

@@ -31,11 +31,11 @@ GPSIMD_TILES = 3
 FLOPS = 2 * NODES * NEIGHBOURS * K * WIDTH + 2 * NODES * K * WIDTH
 
 
-def quantise_weight(nc, pool, raw, codes, scales):
+def quantise_weight(nc, copy, pool, raw, codes, scales):
     grouped = []
     for g in range(PASSES):
         tile_g = pool.tile([P, WIDTH * PACK], BF16, align_bytes=64, name="w_grouped_%d" % g)
-        nc.vector.tensor_copy(
+        copy(
             out=tile_g[:].rearrange("p (c i t) -> p c t i", i=4, t=PACK),
             in_=raw[:, g * PACK : (g + 1) * PACK, :].rearrange("p t (c i) -> p c t i", i=4),
         )
@@ -63,33 +63,35 @@ def tile_graph_gan_pb_kernel(tc, e2, x, fe_w2, fe_b2, fn_w0, fn_b0, out):
 
         b2_rows = keep.tile([P, P], BF16)
         nc.vector.memset(b2_rows[:], 0.0)
-        nc.scalar.dma_start(out=b2_rows[0:F_TILES, :], in_=fe_b2.rearrange("(t p) -> t p", p=P))
-        x_sb = keep.tile([P, K_PASS], BF16)
-        nc.scalar.dma_start(out=x_sb[:], in_=x.rearrange("b i d -> (b i) d"))
-
         w1_raw = keep.tile([P, PASSES * PACK, WIDTH], BF16)
         nc.sync.dma_start(
             out=w1_raw[:].rearrange("p (a e) c -> p a e c", e=2),
             in_=fe_w2.rearrange("(a p e) c -> p a e c", p=P, e=2),
         )
+        nc.sync.dma_start(out=b2_rows[0:F_TILES, :], in_=fe_b2.rearrange("(t p) -> t p", p=P))
         e2_rows = e2.rearrange("b i j k -> (b i) (j k)")
         e2_sb = []
+        x_sb = keep.tile([P, K_PASS], BF16)
         w0_raw = keep.tile([P, PASSES * PACK, WIDTH], BF16)
         for c in range(CHUNKS):
             e2_c = keep.tile([P, J_CHUNK * K], BF16, name="e2_%d" % c)
-            nc.sync.dma_start(out=e2_c[:], in_=e2_rows[:, c * J_CHUNK * K : (c + 1) * J_CHUNK * K])
+            pieces = J_CHUNK if c == 0 else 1
+            run = J_CHUNK * K // pieces
+            for i in range(pieces):
+                first = c * J_CHUNK * K + i * run
+                nc.sync.dma_start(
+                    out=e2_c[:, i * run : (i + 1) * run], in_=e2_rows[:, first : first + run]
+                )
             e2_sb.append(e2_c)
-            if c == 0:
+            if c == 1:
+                nc.sync.dma_start(out=x_sb[:], in_=x.rearrange("b i d -> (b i) d"))
                 nc.sync.dma_start(out=w0_raw[:], in_=fn_w0.rearrange("(a p) c -> p a c", p=P))
         b0_all = keep.tile([P, WIDTH], BF16)
         nc.sync.dma_start(out=b0_all[:], in_=fn_b0.partition_broadcast(P))
 
         w1_codes = keep.tile([P, PASSES, WIDTH], U32, align_bytes=64)
         w1_scales = keep.tile([P, PASSES, WIDTH], U8, align_bytes=64)
-        quantise_weight(nc, w_stage, w1_raw, w1_codes, w1_scales)
-        w0_codes = keep.tile([P, PASSES, WIDTH], U32, align_bytes=64)
-        w0_scales = keep.tile([P, PASSES, WIDTH], U8, align_bytes=64)
-        quantise_weight(nc, w_stage, w0_raw, w0_codes, w0_scales)
+        quantise_weight(nc, nc.vector.tensor_copy, w_stage, w1_raw, w1_codes, w1_scales)
 
         b2_ps = psum_t.tile([P, P], BF16, tag="xt")
         nc.tensor.transpose(b2_ps[:], b2_rows[:], ident_bf16[:])
@@ -113,12 +115,6 @@ def tile_graph_gan_pb_kernel(tc, e2, x, fe_w2, fe_b2, fn_w0, fn_b0, out):
                 scales=h_scales[:, g, :],
                 in_=h_grouped[:, g * NODES * PACK : (g + 1) * NODES * PACK],
             )
-
-        x_ps = psum_t.tile([P, PACK, NODES], BF16, tag="xt")
-        for t in range(PACK):
-            nc.tensor.transpose(x_ps[:, t, :], x_sb[:, t * P : (t + 1) * P], ident_bf16[:])
-        nc.vector.tensor_copy(out=h_view[:, 1, :, :], in_=x_ps[:].rearrange("p t n -> p n t"))
-        quantise_h(1)
 
         def quantise_chunk(c):
             e2_words = e2_sb[c][:].bitcast(F32)
@@ -198,27 +194,36 @@ def tile_graph_gan_pb_kernel(tc, e2, x, fe_w2, fe_b2, fn_w0, fn_b0, out):
             edge_layer(c, ready[0], ready[1])
             ready = following
 
-        for t in range(F_TILES):
-            agg = work.tile([P, NODES], F32)
-            if t < GPSIMD_TILES:
+        w0_codes = keep.tile([P, PASSES, WIDTH], U32, align_bytes=64)
+        w0_scales = keep.tile([P, PASSES, WIDTH], U8, align_bytes=64)
+        quantise_weight(nc, nc.scalar.copy, w_stage, w0_raw, w0_codes, w0_scales)
+        x_ps = psum_t.tile([P, PACK, NODES], BF16, tag="xt")
+        for t in range(PACK):
+            nc.tensor.transpose(x_ps[:, t, :], x_sb[:, t * P : (t + 1) * P], ident_bf16[:])
+        nc.vector.tensor_copy(out=h_view[:, 1, :, :], in_=x_ps[:].rearrange("p t n -> p n t"))
+        quantise_h(1)
+
+        for t in vector_tiles:
+            both = work.tile([P, COLS], F32)
+            nc.vector.scalar_tensor_tensor(
+                out=both[:], in0=clip_sum[t][:], scalar=(1.0 - ALPHA) / ALPHA,
+                in1=v_sum[t][:], op0=ALU.mult, op1=ALU.add,
+            )
+            both_sum = work.tile([P, NODES], F32)
+            nc.vector.tensor_reduce(
+                out=both_sum[:], in_=both[:].rearrange("p (j n) -> p n j", j=J_CHUNK),
+                axis=AXIS.X, op=ALU.add,
+            )
+            nc.vector.tensor_scalar(
+                out=h_view[:, 0, :, t], in0=both_sum[:], scalar1=ALPHA,
+                scalar2=b2_all_j[:, t : t + 1], op0=ALU.mult, op1=ALU.add,
+            )
+        with nc.allow_low_precision(reason="the sum is float32; its one rounding to bfloat16 is h's"):
+            for t in range(GPSIMD_TILES):
                 nc.vector.tensor_reduce(
-                    out=agg[:], in_=a3_sum[t][:].rearrange("p (j n) -> p n j", j=J_CHUNK),
+                    out=h_view[:, 0, :, t],
+                    in_=a3_sum[t][:].rearrange("p (j n) -> p n j", j=J_CHUNK),
                     axis=AXIS.X, op=ALU.add,
-                )
-                nc.vector.tensor_copy(out=h_view[:, 0, :, t], in_=agg[:])
-            else:
-                both = work.tile([P, COLS], F32)
-                nc.vector.scalar_tensor_tensor(
-                    out=both[:], in0=clip_sum[t][:], scalar=(1.0 - ALPHA) / ALPHA,
-                    in1=v_sum[t][:], op0=ALU.mult, op1=ALU.add,
-                )
-                nc.vector.tensor_reduce(
-                    out=agg[:], in_=both[:].rearrange("p (j n) -> p n j", j=J_CHUNK),
-                    axis=AXIS.X, op=ALU.add,
-                )
-                nc.vector.tensor_scalar(
-                    out=h_view[:, 0, :, t], in0=agg[:], scalar1=ALPHA,
-                    scalar2=b2_all_j[:, t : t + 1], op0=ALU.mult, op1=ALU.add,
                 )
         quantise_h(0)
 
@@ -233,10 +238,17 @@ def tile_graph_gan_pb_kernel(tc, e2, x, fe_w2, fe_b2, fn_w0, fn_b0, out):
                 start=(g == 0),
                 stop=(g == PASSES - 1),
             )
-        biased = keep.tile([P, WIDTH], F32)
-        nc.vector.tensor_tensor(out=biased[:], in0=out_ps[:], in1=b0_all[:], op=ALU.add)
-        result = keep.tile([P, WIDTH], F32)
-        nc.vector.scalar_tensor_tensor(
-            out=result[:], in0=biased[:], scalar=ALPHA, in1=biased[:], op0=ALU.mult, op1=ALU.max
-        )
-        nc.sync.dma_start(out=out.rearrange("b i g -> (b i) g"), in_=result[:])
+        out_rows = out.rearrange("b i g -> (b i) g")
+        half = WIDTH // 2
+        for i, queue in enumerate((nc.sync, nc.scalar)):
+            cols = slice(i * half, (i + 1) * half)
+            biased = work.tile([P, half], F32)
+            nc.vector.tensor_tensor(
+                out=biased[:], in0=out_ps[:, cols], in1=b0_all[:, cols], op=ALU.add
+            )
+            result = work.tile([P, half], F32)
+            nc.vector.scalar_tensor_tensor(
+                out=result[:], in0=biased[:], scalar=ALPHA, in1=biased[:],
+                op0=ALU.mult, op1=ALU.max,
+            )
+            queue.dma_start(out=out_rows[:, cols], in_=result[:])

@@ -53,8 +53,9 @@ def tile_graph_gan_pb_kernel(tc, e2, x, fe_w2, fe_b2, fn_w0, fn_b0, out):
         w_stage = stack.enter_context(tc.tile_pool(name="w_stage", bufs=2))
         stage = stack.enter_context(tc.tile_pool(name="stage", bufs=3))
         work = stack.enter_context(tc.tile_pool(name="work", bufs=4))
-        psum_t = stack.enter_context(tc.psum_pool(name="psum_t", bufs=4))
+        psum_t = stack.enter_context(tc.psum_pool(name="psum_t", bufs=3))
         psum_acc = stack.enter_context(tc.psum_pool(name="psum_acc", bufs=4))
+        psum_keep = stack.enter_context(tc.psum_pool(name="psum_keep", bufs=1))
 
         ident_f32 = keep.tile([P, P], F32)
         make_identity(nc, ident_f32[:])
@@ -142,23 +143,26 @@ def tile_graph_gan_pb_kernel(tc, e2, x, fe_w2, fe_b2, fn_w0, fn_b0, out):
 
         a3_sum = [keep.tile([P, COLS], F32, name="a3_sum_%d" % t) for t in range(GPSIMD_TILES)]
         vector_tiles = range(GPSIMD_TILES, F_TILES)
-        v_sum = dict((t, keep.tile([P, COLS], F32, name="v_sum_%d" % t)) for t in vector_tiles)
+        v_sum = dict((t, psum_keep.tile([P, COLS], F32, name="v_sum_%d" % t)) for t in vector_tiles)
         clip_sum = dict((t, keep.tile([P, COLS], F32, name="clip_sum_%d" % t)) for t in vector_tiles)
 
         def edge_layer(c, codes, scales):
-            for t in range(F_TILES):
+            def multiply(bank, t, g, start, stop):
                 f_cols = slice(t * P, (t + 1) * P)
+                nc.tensor.matmul_mx(
+                    out=bank[:],
+                    lhsT=w1_codes[:, g, f_cols].bitcast(FP8X4),
+                    lhsT_scale=w1_scales[:, g, f_cols],
+                    rhs=codes[:, g, :].bitcast(FP8X4),
+                    rhs_scale=scales[:, g, :],
+                    start=start,
+                    stop=stop,
+                )
+
+            for t in range(F_TILES):
                 acc = psum_acc.tile([P, COLS], F32)
                 for g in range(PASSES):
-                    nc.tensor.matmul_mx(
-                        out=acc[:],
-                        lhsT=w1_codes[:, g, f_cols].bitcast(FP8X4),
-                        lhsT_scale=w1_scales[:, g, f_cols],
-                        rhs=codes[:, g, :].bitcast(FP8X4),
-                        rhs_scale=scales[:, g, :],
-                        start=(g == 0),
-                        stop=(g == PASSES - 1),
-                    )
+                    multiply(acc, t, g, g == 0, g == PASSES - 1)
                 if t < GPSIMD_TILES:
                     scaled = work.tile([P, COLS], F32)
                     nc.scalar.activation(
@@ -174,15 +178,16 @@ def tile_graph_gan_pb_kernel(tc, e2, x, fe_w2, fe_b2, fn_w0, fn_b0, out):
                         nc.gpsimd.tensor_tensor(
                             out=a3_sum[t][:], in0=a3_sum[t][:], in1=a3[:], op=ALU.add
                         )
-                elif c == 0:
-                    nc.vector.tensor_copy(out=v_sum[t][:], in_=acc[:])
+                    continue
+                for g in range(PASSES):
+                    multiply(
+                        v_sum[t], t, g, c == 0 and g == 0, c == CHUNKS - 1 and g == PASSES - 1
+                    )
+                if c == 0:
                     nc.vector.tensor_scalar_max(
                         out=clip_sum[t][:], in0=acc[:], scalar1=b2_neg[:, t : t + 1]
                     )
                 else:
-                    nc.vector.tensor_tensor(
-                        out=v_sum[t][:], in0=acc[:], in1=v_sum[t][:], op=ALU.add
-                    )
                     nc.vector.scalar_tensor_tensor(
                         out=clip_sum[t][:], in0=acc[:], scalar=b2_neg[:, t : t + 1],
                         in1=clip_sum[t][:], op0=ALU.max, op1=ALU.add,

@@ -26,57 +26,54 @@ CHUNKS = NEIGHBOURS // J_CHUNK
 COLS = J_CHUNK * NODES
 WORD_BLOCKS = K // 2 // P
 ALPHA = 0.2
-GPSIMD_TILES = 3
+GPSIMD_TILES = (0, 1)
+TENSOR_TILES = (2,)
+VECTOR_TILES = (3,)
+PSUM_BANKS = 8
+AGG_PASS, X_PASS = 0, 1
 
 FLOPS = 2 * NODES * NEIGHBOURS * K * WIDTH + 2 * NODES * K * WIDTH
 
 
-def quantise_weight(nc, copy, pool, raw, codes, scales):
-    grouped = []
-    for g in range(PASSES):
-        tile_g = pool.tile([P, WIDTH * PACK], BF16, align_bytes=64, name="w_grouped_%d" % g)
-        copy(
-            out=tile_g[:].rearrange("p (c i t) -> p c t i", i=4, t=PACK),
-            in_=raw[:, g * PACK : (g + 1) * PACK, :].rearrange("p t (c i) -> p c t i", i=4),
-        )
-        grouped.append(tile_g)
-    for g in range(PASSES):
-        nc.vector.quantize_mx(
-            out=codes[:, g, :].bitcast(FP8X4), scales=scales[:, g, :], in_=grouped[g][:]
-        )
+def regroup(copy, raw, grouped, g):
+    copy(
+        out=grouped[g][:].rearrange("p (c i t) -> p c t i", i=4, t=PACK),
+        in_=raw[:, g * PACK : (g + 1) * PACK, :].rearrange("p t (c i) -> p c t i", i=4),
+    )
 
 
 def tile_graph_gan_pb_kernel(tc, e2, x, fe_w2, fe_b2, fn_w0, fn_b0, out):
     nc = tc.nc
     with ExitStack() as stack:
+        stack.enter_context(tc.manual_schedule())
         keep = stack.enter_context(tc.tile_pool(name="keep", bufs=1))
-        w_stage = stack.enter_context(tc.tile_pool(name="w_stage", bufs=2))
         stage = stack.enter_context(tc.tile_pool(name="stage", bufs=3))
         work = stack.enter_context(tc.tile_pool(name="work", bufs=4))
-        psum_t = stack.enter_context(tc.psum_pool(name="psum_t", bufs=3))
-        psum_acc = stack.enter_context(tc.psum_pool(name="psum_acc", bufs=4))
-        psum_keep = stack.enter_context(tc.psum_pool(name="psum_keep", bufs=1))
-
-        ident_f32 = keep.tile([P, P], F32)
-        make_identity(nc, ident_f32[:])
-        ident_bf16 = keep.tile([P, P], BF16)
-        make_identity(nc, ident_bf16[:])
+        psum_keep = stack.enter_context(tc.psum_pool(name="psum_keep", bufs=len(TENSOR_TILES)))
+        banks = stack.enter_context(
+            tc.psum_pool(name="banks", bufs=PSUM_BANKS - len(TENSOR_TILES))
+        )
 
         b2_rows = keep.tile([P, P], BF16)
         nc.vector.memset(b2_rows[:], 0.0)
+        ident_bf16 = keep.tile([P, P], BF16)
+        make_identity(nc, ident_bf16[:])
+        ident_f32 = keep.tile([P, P], F32)
+        make_identity(nc, ident_f32[:])
+
+        x_sb = keep.tile([P, K_PASS], BF16)
+        nc.sync.dma_start(out=x_sb[:], in_=x.rearrange("b i d -> (b i) d"))
+        nc.sync.dma_start(out=b2_rows[0:F_TILES, :], in_=fe_b2.rearrange("(t p) -> t p", p=P))
         w1_raw = keep.tile([P, PASSES * PACK, WIDTH], BF16)
         nc.sync.dma_start(
             out=w1_raw[:].rearrange("p (a e) c -> p a e c", e=2),
             in_=fe_w2.rearrange("(a p e) c -> p a e c", p=P, e=2),
         )
-        nc.sync.dma_start(out=b2_rows[0:F_TILES, :], in_=fe_b2.rearrange("(t p) -> t p", p=P))
         e2_rows = e2.rearrange("b i j k -> (b i) (j k)")
         e2_sb = []
-        x_sb = keep.tile([P, K_PASS], BF16)
-        w0_raw = keep.tile([P, PASSES * PACK, WIDTH], BF16)
         for c in range(CHUNKS):
             e2_c = keep.tile([P, J_CHUNK * K], BF16, name="e2_%d" % c)
-            pieces = J_CHUNK if c == 0 else 1
+            pieces = max(1, J_CHUNK >> c)
             run = J_CHUNK * K // pieces
             for i in range(pieces):
                 first = c * J_CHUNK * K + i * run
@@ -84,26 +81,10 @@ def tile_graph_gan_pb_kernel(tc, e2, x, fe_w2, fe_b2, fn_w0, fn_b0, out):
                     out=e2_c[:, i * run : (i + 1) * run], in_=e2_rows[:, first : first + run]
                 )
             e2_sb.append(e2_c)
-            if c == 1:
-                nc.sync.dma_start(out=x_sb[:], in_=x.rearrange("b i d -> (b i) d"))
-                nc.sync.dma_start(out=w0_raw[:], in_=fn_w0.rearrange("(a p) c -> p a c", p=P))
+        w0_raw = keep.tile([P, PASSES * PACK, WIDTH], BF16)
+        nc.sync.dma_start(out=w0_raw[:], in_=fn_w0.rearrange("(a p) c -> p a c", p=P))
         b0_all = keep.tile([P, WIDTH], BF16)
         nc.sync.dma_start(out=b0_all[:], in_=fn_b0.partition_broadcast(P))
-
-        w1_codes = keep.tile([P, PASSES, WIDTH], U32, align_bytes=64)
-        w1_scales = keep.tile([P, PASSES, WIDTH], U8, align_bytes=64)
-        quantise_weight(nc, nc.vector.tensor_copy, w_stage, w1_raw, w1_codes, w1_scales)
-
-        b2_ps = psum_t.tile([P, P], BF16, tag="xt")
-        nc.tensor.transpose(b2_ps[:], b2_rows[:], ident_bf16[:])
-        b2 = keep.tile([P, F_TILES], F32)
-        nc.vector.tensor_copy(out=b2[:], in_=b2_ps[:, 0:F_TILES])
-        b2_alpha = keep.tile([P, F_TILES], F32)
-        nc.vector.tensor_scalar_mul(out=b2_alpha[:], in0=b2[:], scalar1=ALPHA)
-        b2_neg = keep.tile([P, F_TILES], F32)
-        nc.vector.tensor_scalar_mul(out=b2_neg[:], in0=b2[:], scalar1=-1.0)
-        b2_all_j = keep.tile([P, F_TILES], F32)
-        nc.vector.tensor_scalar_mul(out=b2_all_j[:], in0=b2[:], scalar1=float(NEIGHBOURS))
 
         h_grouped = keep.tile([P, PASSES * NODES * PACK], BF16, align_bytes=64)
         h_view = h_grouped[:].rearrange("p (g n t) -> p g n t", g=PASSES, t=PACK)
@@ -117,6 +98,46 @@ def tile_graph_gan_pb_kernel(tc, e2, x, fe_w2, fe_b2, fn_w0, fn_b0, out):
                 in_=h_grouped[:, g * NODES * PACK : (g + 1) * NODES * PACK],
             )
 
+        x_ps = banks.tile([P, PACK, NODES], BF16, tag="bank")
+        for t in range(PACK):
+            nc.tensor.transpose(x_ps[:, t, :], x_sb[:, t * P : (t + 1) * P], ident_bf16[:])
+        nc.vector.tensor_copy(
+            out=h_view[:, X_PASS, :, :], in_=x_ps[:].rearrange("p t n -> p n t")
+        )
+        quantise_h(X_PASS)
+
+        b2_ps = banks.tile([P, P], BF16, tag="bank")
+        nc.tensor.transpose(b2_ps[:], b2_rows[:], ident_bf16[:])
+        b2 = keep.tile([P, F_TILES], F32)
+        nc.vector.tensor_copy(out=b2[:], in_=b2_ps[:, 0:F_TILES])
+        b2_alpha = keep.tile([P, F_TILES], F32)
+        nc.vector.tensor_scalar_mul(out=b2_alpha[:], in0=b2[:], scalar1=ALPHA)
+        b2_neg = keep.tile([P, F_TILES], F32)
+        nc.vector.tensor_scalar_mul(out=b2_neg[:], in0=b2[:], scalar1=-1.0)
+        b2_column = keep.tile([P, F_TILES], F32)
+        nc.vector.tensor_scalar_mul(out=b2_column[:], in0=b2[:], scalar1=float(CHUNKS))
+
+        def weight_tiles(name):
+            grouped = [
+                keep.tile([P, WIDTH * PACK], BF16, align_bytes=64, name="%s_grouped_%d" % (name, g))
+                for g in range(PASSES)
+            ]
+            codes = keep.tile([P, PASSES, WIDTH], U32, align_bytes=64, name="%s_codes" % name)
+            scales = keep.tile([P, PASSES, WIDTH], U8, align_bytes=64, name="%s_scales" % name)
+            return grouped, codes, scales
+
+        def quantise_weight(grouped, codes, scales):
+            for g in range(PASSES):
+                nc.vector.quantize_mx(
+                    out=codes[:, g, :].bitcast(FP8X4), scales=scales[:, g, :], in_=grouped[g][:]
+                )
+
+        w1_grouped, w1_codes, w1_scales = weight_tiles("w1")
+        for g in range(PASSES):
+            regroup(nc.vector.tensor_copy, w1_raw, w1_grouped, g)
+        quantise_weight(w1_grouped, w1_codes, w1_scales)
+        w0_grouped, w0_codes, w0_scales = weight_tiles("w0")
+
         def quantise_chunk(c):
             e2_words = e2_sb[c][:].bitcast(F32)
             grouped = stage.tile([P, PASSES * COLS * PACK], BF16, align_bytes=64)
@@ -124,7 +145,7 @@ def tile_graph_gan_pb_kernel(tc, e2, x, fe_w2, fe_b2, fn_w0, fn_b0, out):
                 "p (g j n u) -> p g j n u", g=PASSES, j=J_CHUNK, u=2
             )
             for j in range(J_CHUNK):
-                xt = psum_t.tile([P, WORD_BLOCKS, NODES], F32)
+                xt = banks.tile([P, WORD_BLOCKS, NODES], F32, tag="bank")
                 for w in range(WORD_BLOCKS):
                     first = (j * WORD_BLOCKS + w) * P
                     nc.tensor.transpose(xt[:, w, :], e2_words[:, first : first + P], ident_f32[:])
@@ -141,10 +162,16 @@ def tile_graph_gan_pb_kernel(tc, e2, x, fe_w2, fe_b2, fn_w0, fn_b0, out):
             )
             return codes, scales
 
-        a3_sum = [keep.tile([P, COLS], F32, name="a3_sum_%d" % t) for t in range(GPSIMD_TILES)]
-        vector_tiles = range(GPSIMD_TILES, F_TILES)
-        v_sum = dict((t, psum_keep.tile([P, COLS], F32, name="v_sum_%d" % t)) for t in vector_tiles)
-        clip_sum = dict((t, keep.tile([P, COLS], F32, name="clip_sum_%d" % t)) for t in vector_tiles)
+        a3_sum = dict((t, keep.tile([P, COLS], F32, name="a3_sum_%d" % t)) for t in GPSIMD_TILES)
+        clip_sum = dict(
+            (t, keep.tile([P, COLS], F32, name="clip_sum_%d" % t))
+            for t in TENSOR_TILES + VECTOR_TILES
+        )
+        line_sum = dict(
+            (t, keep.tile([P, COLS], F32, name="line_sum_%d" % t))
+            for t in TENSOR_TILES + VECTOR_TILES
+        )
+        v_sum = dict((t, psum_keep.tile([P, COLS], F32, name="v_sum_%d" % t)) for t in TENSOR_TILES)
 
         def edge_layer(c, codes, scales):
             def multiply(bank, t, g, start, stop):
@@ -160,10 +187,15 @@ def tile_graph_gan_pb_kernel(tc, e2, x, fe_w2, fe_b2, fn_w0, fn_b0, out):
                 )
 
             for t in range(F_TILES):
-                acc = psum_acc.tile([P, COLS], F32)
+                if t in TENSOR_TILES:
+                    for g in range(PASSES):
+                        multiply(
+                            v_sum[t], t, g, c == 0 and g == 0, c == CHUNKS - 1 and g == PASSES - 1
+                        )
+                acc = banks.tile([P, COLS], F32, tag="bank")
                 for g in range(PASSES):
                     multiply(acc, t, g, g == 0, g == PASSES - 1)
-                if t < GPSIMD_TILES:
+                if t in GPSIMD_TILES:
                     scaled = work.tile([P, COLS], F32)
                     nc.scalar.activation(
                         out=scaled[:], in_=acc[:], func=ACT.Identity,
@@ -179,10 +211,17 @@ def tile_graph_gan_pb_kernel(tc, e2, x, fe_w2, fe_b2, fn_w0, fn_b0, out):
                             out=a3_sum[t][:], in0=a3_sum[t][:], in1=a3[:], op=ALU.add
                         )
                     continue
-                for g in range(PASSES):
-                    multiply(
-                        v_sum[t], t, g, c == 0 and g == 0, c == CHUNKS - 1 and g == PASSES - 1
-                    )
+                if t in VECTOR_TILES:
+                    if c == 0:
+                        nc.vector.tensor_scalar(
+                            out=line_sum[t][:], in0=acc[:], scalar1=ALPHA,
+                            scalar2=b2_column[:, t : t + 1], op0=ALU.mult, op1=ALU.add,
+                        )
+                    else:
+                        nc.vector.scalar_tensor_tensor(
+                            out=line_sum[t][:], in0=acc[:], scalar=ALPHA, in1=line_sum[t][:],
+                            op0=ALU.mult, op1=ALU.add,
+                        )
                 if c == 0:
                     nc.vector.tensor_scalar_max(
                         out=clip_sum[t][:], in0=acc[:], scalar1=b2_neg[:, t : t + 1]
@@ -198,51 +237,53 @@ def tile_graph_gan_pb_kernel(tc, e2, x, fe_w2, fe_b2, fn_w0, fn_b0, out):
             following = quantise_chunk(c + 1) if c + 1 < CHUNKS else None
             edge_layer(c, ready[0], ready[1])
             ready = following
-
-        w0_codes = keep.tile([P, PASSES, WIDTH], U32, align_bytes=64)
-        w0_scales = keep.tile([P, PASSES, WIDTH], U8, align_bytes=64)
-        quantise_weight(nc, nc.scalar.copy, w_stage, w0_raw, w0_codes, w0_scales)
-        x_ps = psum_t.tile([P, PACK, NODES], BF16, tag="xt")
-        for t in range(PACK):
-            nc.tensor.transpose(x_ps[:, t, :], x_sb[:, t * P : (t + 1) * P], ident_bf16[:])
-        nc.vector.tensor_copy(out=h_view[:, 1, :, :], in_=x_ps[:].rearrange("p t n -> p n t"))
-        quantise_h(1)
-
-        for t in vector_tiles:
-            both = work.tile([P, COLS], F32)
-            nc.vector.scalar_tensor_tensor(
-                out=both[:], in0=clip_sum[t][:], scalar=(1.0 - ALPHA) / ALPHA,
-                in1=v_sum[t][:], op0=ALU.mult, op1=ALU.add,
+            g = c - (CHUNKS - PASSES)
+            if g >= 0:
+                regroup(nc.scalar.copy, w0_raw, w0_grouped, g)
+        for t in TENSOR_TILES:
+            nc.scalar.activation(
+                out=line_sum[t][:], in_=v_sum[t][:], func=ACT.Identity,
+                bias=b2_column[:, t : t + 1], scale=ALPHA,
             )
-            both_sum = work.tile([P, NODES], F32)
-            nc.vector.tensor_reduce(
-                out=both_sum[:], in_=both[:].rearrange("p (j n) -> p n j", j=J_CHUNK),
-                axis=AXIS.X, op=ALU.add,
-            )
-            nc.vector.tensor_scalar(
-                out=h_view[:, 0, :, t], in0=both_sum[:], scalar1=ALPHA,
-                scalar2=b2_all_j[:, t : t + 1], op0=ALU.mult, op1=ALU.add,
-            )
-        with nc.allow_low_precision(reason="the sum is float32; its one rounding to bfloat16 is h's"):
-            for t in range(GPSIMD_TILES):
-                nc.vector.tensor_reduce(
-                    out=h_view[:, 0, :, t],
-                    in_=a3_sum[t][:].rearrange("p (j n) -> p n j", j=J_CHUNK),
-                    axis=AXIS.X, op=ALU.add,
-                )
-        quantise_h(0)
+        quantise_weight(w0_grouped, w0_codes, w0_scales)
 
-        out_ps = psum_acc.tile([P, WIDTH], F32, tag="acc")
-        for g in range(PASSES):
+        out_ps = banks.tile([P, WIDTH], F32, tag="bank")
+
+        def node_layer(g, start, stop):
             nc.tensor.matmul_mx(
                 out=out_ps[:],
                 lhsT=h_codes[:, g, :].bitcast(FP8X4),
                 lhsT_scale=h_scales[:, g, :],
                 rhs=w0_codes[:, g, :].bitcast(FP8X4),
                 rhs_scale=w0_scales[:, g, :],
-                start=(g == 0),
-                stop=(g == PASSES - 1),
+                start=start,
+                stop=stop,
             )
+
+        node_layer(X_PASS, True, False)
+
+        def join_sums(t):
+            both = work.tile([P, COLS], F32)
+            nc.vector.scalar_tensor_tensor(
+                out=both[:], in0=clip_sum[t][:], scalar=1.0 - ALPHA, in1=line_sum[t][:],
+                op0=ALU.mult, op1=ALU.add,
+            )
+            return both
+
+        a3_cols = dict(
+            [(t, join_sums(t)) for t in TENSOR_TILES + VECTOR_TILES]
+            + [(t, a3_sum[t]) for t in GPSIMD_TILES]
+        )
+        with nc.allow_low_precision(reason="the sum is float32; its one rounding to bfloat16 is h's"):
+            for t in TENSOR_TILES + VECTOR_TILES + GPSIMD_TILES:
+                nc.vector.tensor_reduce(
+                    out=h_view[:, AGG_PASS, :, t],
+                    in_=a3_cols[t][:].rearrange("p (j n) -> p n j", j=J_CHUNK),
+                    axis=AXIS.X, op=ALU.add,
+                )
+        quantise_h(AGG_PASS)
+        node_layer(AGG_PASS, False, True)
+
         out_rows = out.rearrange("b i g -> (b i) g")
         half = WIDTH // 2
         for i, queue in enumerate((nc.sync, nc.scalar)):

@@ -286,7 +286,7 @@ def tile_graph_gan_pb_kernel(tc, e2, x, fe_w2, fe_b2, fn_w0, fn_b0, out):
 
         out_rows = out.rearrange("b i g -> (b i) g")
         half = WIDTH // 2
-        for i, queue in enumerate((nc.sync, nc.scalar)):
+        for i in range(WIDTH // half):
             cols = slice(i * half, (i + 1) * half)
             biased = work.tile([P, half], F32)
             nc.vector.tensor_tensor(
@@ -297,4 +297,4 @@ def tile_graph_gan_pb_kernel(tc, e2, x, fe_w2, fe_b2, fn_w0, fn_b0, out):
                 out=result[:], in0=biased[:], scalar=ALPHA, in1=biased[:],
                 op0=ALU.mult, op1=ALU.max,
             )
-            queue.dma_start(out=out_rows[:, cols], in_=result[:])
+            nc.sync.dma_start(out=out_rows[:, cols], in_=result[:])

@@ -45,7 +45,6 @@ def regroup(copy, raw, grouped, g):
 def tile_graph_gan_pb_kernel(tc, e2, x, fe_w2, fe_b2, fn_w0, fn_b0, out):
     nc = tc.nc
     with ExitStack() as stack:
-        stack.enter_context(tc.manual_schedule())
         keep = stack.enter_context(tc.tile_pool(name="keep", bufs=1))
         stage = stack.enter_context(tc.tile_pool(name="stage", bufs=3))
         work = stack.enter_context(tc.tile_pool(name="work", bufs=4))

from contextlib import ExitStack

import concourse.mybir as mybir
from concourse.masks import make_identity

F32 = mybir.dt.float32
BF16 = mybir.dt.bfloat16
U32 = mybir.dt.uint32
U8 = mybir.dt.uint8
FP8X4 = mybir.dt.float8_e4m3fn_x4
ALU = mybir.AluOpType
ACT = mybir.ActivationFunctionType
AXIS = mybir.AxisListType

P = 128
PACK = 4
K_PASS = P * PACK
NODES = 128
NEIGHBOURS = 32
K = 1024
PASSES = K // K_PASS
WIDTH = 512
F_TILES = WIDTH // P
J_CHUNK = 4
CHUNKS = NEIGHBOURS // J_CHUNK
COLS = J_CHUNK * NODES
WORD_BLOCKS = K // 2 // P
ALPHA = 0.2
GPSIMD_TILES = (0, 1)
TENSOR_TILES = (2,)
VECTOR_TILES = (3,)
PSUM_BANKS = 8
AGG_PASS, X_PASS = 0, 1

FLOPS = 2 * NODES * NEIGHBOURS * K * WIDTH + 2 * NODES * K * WIDTH


def regroup(copy, raw, grouped, g):
    copy(
        out=grouped[g][:].rearrange("p (c i t) -> p c t i", i=4, t=PACK),
        in_=raw[:, g * PACK : (g + 1) * PACK, :].rearrange("p t (c i) -> p c t i", i=4),
    )


def tile_graph_gan_pb_kernel(tc, e2, x, fe_w2, fe_b2, fn_w0, fn_b0, out):
    nc = tc.nc
    with ExitStack() as stack:
        keep = stack.enter_context(tc.tile_pool(name="keep", bufs=1))
        stage = stack.enter_context(tc.tile_pool(name="stage", bufs=3))
        work = stack.enter_context(tc.tile_pool(name="work", bufs=4))
        psum_keep = stack.enter_context(tc.psum_pool(name="psum_keep", bufs=len(TENSOR_TILES)))
        banks = stack.enter_context(
            tc.psum_pool(name="banks", bufs=PSUM_BANKS - len(TENSOR_TILES))
        )

        b2_rows = keep.tile([P, P], BF16)
        nc.vector.memset(b2_rows[:], 0.0)
        ident_bf16 = keep.tile([P, P], BF16)
        make_identity(nc, ident_bf16[:])
        ident_f32 = keep.tile([P, P], F32)
        make_identity(nc, ident_f32[:])

        x_sb = keep.tile([P, K_PASS], BF16)
        nc.sync.dma_start(out=x_sb[:], in_=x.rearrange("b i d -> (b i) d"))
        nc.sync.dma_start(out=b2_rows[0:F_TILES, :], in_=fe_b2.rearrange("(t p) -> t p", p=P))
        w1_raw = keep.tile([P, PASSES * PACK, WIDTH], BF16)
        nc.sync.dma_start(
            out=w1_raw[:].rearrange("p (a e) c -> p a e c", e=2),
            in_=fe_w2.rearrange("(a p e) c -> p a e c", p=P, e=2),
        )
        e2_rows = e2.rearrange("b i j k -> (b i) (j k)")
        e2_sb = []
        for c in range(CHUNKS):
            e2_c = keep.tile([P, J_CHUNK * K], BF16, name="e2_%d" % c)
            pieces = max(1, J_CHUNK >> c)
            run = J_CHUNK * K // pieces
            for i in range(pieces):
                first = c * J_CHUNK * K + i * run
                nc.sync.dma_start(
                    out=e2_c[:, i * run : (i + 1) * run], in_=e2_rows[:, first : first + run]
                )
            e2_sb.append(e2_c)
        w0_raw = keep.tile([P, PASSES * PACK, WIDTH], BF16)
        nc.sync.dma_start(out=w0_raw[:], in_=fn_w0.rearrange("(a p) c -> p a c", p=P))
        b0_all = keep.tile([P, WIDTH], BF16)
        nc.sync.dma_start(out=b0_all[:], in_=fn_b0.partition_broadcast(P))

        h_grouped = keep.tile([P, PASSES * NODES * PACK], BF16, align_bytes=64)
        h_view = h_grouped[:].rearrange("p (g n t) -> p g n t", g=PASSES, t=PACK)
        h_codes = keep.tile([P, PASSES, NODES], U32, align_bytes=64)
        h_scales = keep.tile([P, PASSES, NODES], U8, align_bytes=64)

        def quantise_h(g):
            nc.vector.quantize_mx(
                out=h_codes[:, g, :].bitcast(FP8X4),
                scales=h_scales[:, g, :],
                in_=h_grouped[:, g * NODES * PACK : (g + 1) * NODES * PACK],
            )

        x_ps = banks.tile([P, PACK, NODES], BF16, tag="bank")
        for t in range(PACK):
            nc.tensor.transpose(x_ps[:, t, :], x_sb[:, t * P : (t + 1) * P], ident_bf16[:])
        nc.vector.tensor_copy(
            out=h_view[:, X_PASS, :, :], in_=x_ps[:].rearrange("p t n -> p n t")
        )
        quantise_h(X_PASS)

        b2_ps = banks.tile([P, P], BF16, tag="bank")
        nc.tensor.transpose(b2_ps[:], b2_rows[:], ident_bf16[:])
        b2 = keep.tile([P, F_TILES], F32)
        nc.vector.tensor_copy(out=b2[:], in_=b2_ps[:, 0:F_TILES])
        b2_alpha = keep.tile([P, F_TILES], F32)
        nc.vector.tensor_scalar_mul(out=b2_alpha[:], in0=b2[:], scalar1=ALPHA)
        b2_neg = keep.tile([P, F_TILES], F32)
        nc.vector.tensor_scalar_mul(out=b2_neg[:], in0=b2[:], scalar1=-1.0)
        b2_column = keep.tile([P, F_TILES], F32)
        nc.vector.tensor_scalar_mul(out=b2_column[:], in0=b2[:], scalar1=float(CHUNKS))

        def weight_tiles(name):
            grouped = [
                keep.tile([P, WIDTH * PACK], BF16, align_bytes=64, name="%s_grouped_%d" % (name, g))
                for g in range(PASSES)
            ]
            codes = keep.tile([P, PASSES, WIDTH], U32, align_bytes=64, name="%s_codes" % name)
            scales = keep.tile([P, PASSES, WIDTH], U8, align_bytes=64, name="%s_scales" % name)
            return grouped, codes, scales

        def quantise_weight(grouped, codes, scales):
            for g in range(PASSES):
                nc.vector.quantize_mx(
                    out=codes[:, g, :].bitcast(FP8X4), scales=scales[:, g, :], in_=grouped[g][:]
                )

        w1_grouped, w1_codes, w1_scales = weight_tiles("w1")
        for g in range(PASSES):
            regroup(nc.vector.tensor_copy, w1_raw, w1_grouped, g)
        quantise_weight(w1_grouped, w1_codes, w1_scales)
        w0_grouped, w0_codes, w0_scales = weight_tiles("w0")

        def quantise_chunk(c):
            e2_words = e2_sb[c][:].bitcast(F32)
            grouped = stage.tile([P, PASSES * COLS * PACK], BF16, align_bytes=64)
            grouped_words = grouped[:].bitcast(F32).rearrange(
                "p (g j n u) -> p g j n u", g=PASSES, j=J_CHUNK, u=2
            )
            for j in range(J_CHUNK):
                xt = banks.tile([P, WORD_BLOCKS, NODES], F32, tag="bank")
                for w in range(WORD_BLOCKS):
                    first = (j * WORD_BLOCKS + w) * P
                    nc.tensor.transpose(xt[:, w, :], e2_words[:, first : first + P], ident_f32[:])
                nc.scalar.copy(
                    out=grouped_words[:, :, j, :, :],
                    in_=xt[:].rearrange("p (g u) n -> p g n u", u=2),
                )
            codes = stage.tile([P, PASSES, COLS], U32, align_bytes=64)
            scales = stage.tile([P, PASSES, COLS], U8, align_bytes=64)
            nc.vector.quantize_mx(
                out=codes[:].rearrange("p g c -> p (g c)").bitcast(FP8X4),
                scales=scales[:].rearrange("p g c -> p (g c)"),
                in_=grouped[:],
            )
            return codes, scales

        a3_sum = dict((t, keep.tile([P, COLS], F32, name="a3_sum_%d" % t)) for t in GPSIMD_TILES)
        clip_sum = dict(
            (t, keep.tile([P, COLS], F32, name="clip_sum_%d" % t))
            for t in TENSOR_TILES + VECTOR_TILES
        )
        line_sum = dict(
            (t, keep.tile([P, COLS], F32, name="line_sum_%d" % t))
            for t in TENSOR_TILES + VECTOR_TILES
        )
        v_sum = dict((t, psum_keep.tile([P, COLS], F32, name="v_sum_%d" % t)) for t in TENSOR_TILES)

        def edge_layer(c, codes, scales):
            def multiply(bank, t, g, start, stop):
                f_cols = slice(t * P, (t + 1) * P)
                nc.tensor.matmul_mx(
                    out=bank[:],
                    lhsT=w1_codes[:, g, f_cols].bitcast(FP8X4),
                    lhsT_scale=w1_scales[:, g, f_cols],
                    rhs=codes[:, g, :].bitcast(FP8X4),
                    rhs_scale=scales[:, g, :],
                    start=start,
                    stop=stop,
                )

            for t in range(F_TILES):
                if t in TENSOR_TILES:
                    for g in range(PASSES):
                        multiply(
                            v_sum[t], t, g, c == 0 and g == 0, c == CHUNKS - 1 and g == PASSES - 1
                        )
                acc = banks.tile([P, COLS], F32, tag="bank")
                for g in range(PASSES):
                    multiply(acc, t, g, g == 0, g == PASSES - 1)
                if t in GPSIMD_TILES:
                    scaled = work.tile([P, COLS], F32)
                    nc.scalar.activation(
                        out=scaled[:], in_=acc[:], func=ACT.Identity,
                        bias=b2_alpha[:, t : t + 1], scale=ALPHA,
                    )
                    a3 = a3_sum[t] if c == 0 else work.tile([P, COLS], F32, name="a3")
                    nc.vector.scalar_tensor_tensor(
                        out=a3[:], in0=acc[:], scalar=b2[:, t : t + 1], in1=scaled[:],
                        op0=ALU.add, op1=ALU.max,
                    )
                    if c > 0:
                        nc.gpsimd.tensor_tensor(
                            out=a3_sum[t][:], in0=a3_sum[t][:], in1=a3[:], op=ALU.add
                        )
                    continue
                if t in VECTOR_TILES:
                    if c == 0:
                        nc.vector.tensor_scalar(
                            out=line_sum[t][:], in0=acc[:], scalar1=ALPHA,
                            scalar2=b2_column[:, t : t + 1], op0=ALU.mult, op1=ALU.add,
                        )
                    else:
                        nc.vector.scalar_tensor_tensor(
                            out=line_sum[t][:], in0=acc[:], scalar=ALPHA, in1=line_sum[t][:],
                            op0=ALU.mult, op1=ALU.add,
                        )
                if c == 0:
                    nc.vector.tensor_scalar_max(
                        out=clip_sum[t][:], in0=acc[:], scalar1=b2_neg[:, t : t + 1]
                    )
                else:
                    nc.vector.scalar_tensor_tensor(
                        out=clip_sum[t][:], in0=acc[:], scalar=b2_neg[:, t : t + 1],
                        in1=clip_sum[t][:], op0=ALU.max, op1=ALU.add,
                    )

        ready = quantise_chunk(0)
        for c in range(CHUNKS):
            following = quantise_chunk(c + 1) if c + 1 < CHUNKS else None
            edge_layer(c, ready[0], ready[1])
            ready = following
            g = c - (CHUNKS - PASSES)
            if g >= 0:
                regroup(nc.scalar.copy, w0_raw, w0_grouped, g)
        for t in TENSOR_TILES:
            nc.scalar.activation(
                out=line_sum[t][:], in_=v_sum[t][:], func=ACT.Identity,
                bias=b2_column[:, t : t + 1], scale=ALPHA,
            )
        quantise_weight(w0_grouped, w0_codes, w0_scales)

        out_ps = banks.tile([P, WIDTH], F32, tag="bank")

        def node_layer(g, start, stop):
            nc.tensor.matmul_mx(
                out=out_ps[:],
                lhsT=h_codes[:, g, :].bitcast(FP8X4),
                lhsT_scale=h_scales[:, g, :],
                rhs=w0_codes[:, g, :].bitcast(FP8X4),
                rhs_scale=w0_scales[:, g, :],
                start=start,
                stop=stop,
            )

        node_layer(X_PASS, True, False)

        def join_sums(t):
            both = work.tile([P, COLS], F32)
            nc.vector.scalar_tensor_tensor(
                out=both[:], in0=clip_sum[t][:], scalar=1.0 - ALPHA, in1=line_sum[t][:],
                op0=ALU.mult, op1=ALU.add,
            )
            return both

        a3_cols = dict(
            [(t, join_sums(t)) for t in TENSOR_TILES + VECTOR_TILES]
            + [(t, a3_sum[t]) for t in GPSIMD_TILES]
        )
        with nc.allow_low_precision(reason="the sum is float32; its one rounding to bfloat16 is h's"):
            for t in TENSOR_TILES + VECTOR_TILES + GPSIMD_TILES:
                nc.vector.tensor_reduce(
                    out=h_view[:, AGG_PASS, :, t],
                    in_=a3_cols[t][:].rearrange("p (j n) -> p n j", j=J_CHUNK),
                    axis=AXIS.X, op=ALU.add,
                )
        quantise_h(AGG_PASS)
        node_layer(AGG_PASS, False, True)

        out_rows = out.rearrange("b i g -> (b i) g")
        half = WIDTH // 2
        for i in range(WIDTH // half):
            cols = slice(i * half, (i + 1) * half)
            biased = work.tile([P, half], F32)
            nc.vector.tensor_tensor(
                out=biased[:], in0=out_ps[:, cols], in1=b0_all[:, cols], op=ALU.add
            )
            result = work.tile([P, half], F32)
            nc.vector.scalar_tensor_tensor(
                out=result[:], in0=biased[:], scalar=ALPHA, in1=biased[:],
                op0=ALU.mult, op1=ALU.max,
            )
            nc.sync.dma_start(out=out_rows[:, cols], in_=result[:])
